import numpy as np
import ml_dtypes


def mxq(x, axis, fmt="e4m3"):
    dtype, down = {"e4m3": (ml_dtypes.float8_e4m3fn, 7), "e5m2": (ml_dtypes.float8_e5m2, 14)}[fmt]
    v = np.moveaxis(np.asarray(x, np.float32).astype(ml_dtypes.bfloat16).astype(np.float64), axis, -1)
    blocks = v.reshape(v.shape[:-1] + (-1, 32))
    amax = np.abs(blocks).max(-1, keepdims=True)
    byte = np.maximum(np.where(amax > 0, np.frexp(amax)[1] - 1 + 127, 0) - down, 1)
    scale = np.exp2(byte - 127.0)
    codes = (blocks / scale).astype(np.float32).astype(dtype).astype(np.float64)
    return np.moveaxis((codes * scale).reshape(v.shape), -1, axis)


WIDE = False


def mx_kscale(k):
    if not WIDE:
        return np.ones(k)
    levels = np.array([10, -10, 5, -5, 0])
    a = np.random.permutation(np.resize(levels, k // 512 * 4)).reshape(k // 512, 4)
    idx = np.arange(k)
    return np.exp2(a[idx // 512, idx % 128 // 32])


BF16 = ml_dtypes.bfloat16


def bf(x):
    return np.asarray(x, np.float32).astype(BF16)


def f64(x):
    return np.asarray(x).astype(np.float64)


E2M1 = np.array([0.0, 0.5, 1.0, 1.5, 2.0, 3.0, 4.0, 6.0, -0.0, -0.5, -1.0, -1.5, -2.0, -3.0, -4.0, -6.0])


def pack_weight(w, fmt):
    k, n = w.shape
    w = f64(bf(w)).reshape(k // 32, 32, n)
    amax = np.abs(w).max(1)
    if fmt == "e4m3":
        byte = np.frexp(amax)[1] - 1 + 127 - 7
    else:
        mant, ex = np.frexp(amax / 6.0)
        byte = np.where(mant > 0.5, ex, ex - 1) + 127
    byte = np.clip(np.where(amax > 0, byte, 1), 1, 254)
    scaled = (w * np.exp2(127.0 - byte)[:, None, :]).reshape(k, n).astype(np.float32)
    by_word = np.ascontiguousarray(scaled.reshape(k // 512, 128, 4, n).transpose(0, 1, 3, 2))
    if fmt == "e4m3":
        words = by_word.astype(ml_dtypes.float8_e4m3fn).view(np.uint8)
    else:
        c = by_word.astype(ml_dtypes.float4_e2m1fn).view(np.uint8) & 0xF
        words = c[..., 0::2] | (c[..., 1::2] << 4)
    return np.ascontiguousarray(words), np.ascontiguousarray(byte.astype(np.uint8).reshape(k // 512, 16, n))


def unpack_weight(words, scales, fmt):
    g, p, n, _ = words.shape
    if fmt == "e4m3":
        vals = np.ascontiguousarray(words).view(ml_dtypes.float8_e4m3fn).astype(np.float64)
    else:
        nib = np.empty((g, p, n, 4), np.uint8)
        nib[..., 0::2] = words & 0xF
        nib[..., 1::2] = words >> 4
        vals = E2M1[nib]
    vals = vals * np.repeat(np.exp2(scales.astype(np.float64) - 127.0), 8, axis=1)[..., None]
    return vals.transpose(0, 1, 3, 2).reshape(g * 512, n)


B, C, T, H, W, AT, AF = 1, 1024, 8, 16, 16, 32, 64
D = C // 2
C2 = 2 * C
NKV = AT * AF
REP, REM = AT // T, AT % T
QS = np.sqrt(2.0 / np.sqrt(D))
FMT = "e4m3"


def setup_inputs():
    s = mx_kscale(C2)
    sa, sv = s[:C], s[C:]
    m = np.random.standard_normal((B, C, T))[..., None, None]
    v = bf((np.random.standard_normal((B, C, T, H, W)) + 0.7 * m) * sv[None, :, None, None, None])
    a = bf(np.random.standard_normal((B, C, AT, AF)) * sa[None, :, None, None])
    Wp = np.random.standard_normal((D, C2)) * 0.8 * QS / np.sqrt(C) / s[None, :]
    Wp_words, Wp_scales = pack_weight(np.ascontiguousarray(Wp.T), FMT)
    bp = bf(np.random.standard_normal(D) * 0.1)
    Wg = np.random.standard_normal((D, C2)) / np.sqrt(C) / s[None, :]
    Wg_words, Wg_scales = pack_weight(np.ascontiguousarray(Wg.T), FMT)
    bg = bf(np.random.standard_normal(D) * 0.1)
    return {"v": v,
            "a": a,
            "Wp_words": Wp_words,
            "Wp_scales": Wp_scales,
            "bp": bp,
            "Wg_words": Wg_words,
            "Wg_scales": Wg_scales,
            "bg": bg}


def reference(v, a, Wp_words, Wp_scales, bp, Wg_words, Wg_scales, bg):
    z = f64(v).mean(axis=(3, 4))
    z = np.repeat(z, REP, axis=2)
    if REM:
        z = np.concatenate([z, np.broadcast_to(z[:, :, -1:], (B, C, REM))], axis=2)
    z = np.broadcast_to(z[..., None], (B, C, AT, AF))
    av = np.concatenate([f64(a), z], axis=1).reshape(B, C2, NKV)
    avq = mxq(av, 1, "e4m3")
    phi_av = (unpack_weight(Wp_words, Wp_scales, FMT).T @ avq) + f64(bp)[:, None]
    g_av = (unpack_weight(Wg_words, Wg_scales, FMT).T @ avq) + f64(bg)[:, None]
    return phi_av, g_av.transpose(0, 2, 1)

@@ -1,0 +1,228 @@
+from contextlib import ExitStack
+
+import concourse.mybir as mybir
+from concourse.masks import make_identity
+
+F32 = mybir.dt.float32
+BF16 = mybir.dt.bfloat16
+I32 = mybir.dt.int32
+U8 = mybir.dt.uint8
+FP8X4 = mybir.dt.float8_e4m3fn_x4
+ADD = mybir.AluOpType.add
+MULT = mybir.AluOpType.mult
+IDENTITY = mybir.ActivationFunctionType.Identity
+
+P = 128
+PACK = 4
+PASSES = 4
+A_PASSES = 2
+Z_PASSES = 2
+STEPS = 8
+PIXELS = 256
+COLS = 2048
+COLS_PER_STEP = COLS // STEPS
+D = 512
+BANK = 512
+HALF = COLS // 2
+CHUNKS = COLS // BANK
+PIXEL_RUN = BANK // STEPS
+Z_COPIES = P // STEPS
+
+FLOPS = 2 * 2 * D * COLS * (PASSES * P * PACK)
+
+
+def tile_nlgate_pa_kernel(tc, v, a, Wp_words, Wp_scales, bp, Wg_words, Wg_scales, bg, out_0, out_1):
+    nc = tc.nc
+    with ExitStack() as ctx:
+        keep = ctx.enter_context(tc.tile_pool(name="keep", bufs=1))
+        stage = ctx.enter_context(tc.tile_pool(name="stage", bufs=2))
+        results = ctx.enter_context(tc.tile_pool(name="results", bufs=4))
+        psum = ctx.enter_context(tc.psum_pool(name="psum", bufs=8))
+
+        ident = keep.tile([P, P], BF16)
+        make_identity(nc, ident[:])
+        ones = keep.tile([P, P], BF16)
+        nc.vector.memset(ones[:], 1.0)
+        bp_rows = keep.tile([P, P], BF16)
+        nc.vector.memset(bp_rows[:], 0.0)
+        bg_rows = keep.tile([P, D], BF16)
+        nc.vector.memset(bg_rows[:], 0.0)
+        wp_planes = keep.tile([P, PASSES, D], U8, align_bytes=64)
+        wg_planes = keep.tile([P, PASSES, D], U8, align_bytes=64)
+        nc.vector.memset(wp_planes[:].bitcast(I32), 0)
+        nc.vector.memset(wg_planes[:].bitcast(I32), 0)
+        z_planes = keep.tile([P, Z_PASSES, P], U8, align_bytes=64)
+        nc.vector.memset(z_planes[:].bitcast(I32), 0)
+
+        v_rows = v[0].rearrange("(g p j) t h w -> g p j (t h w)", p=P, j=PACK)
+        a_rows = a[0].rearrange("(g p j) i f -> g p j (i f)", p=P, j=PACK)
+        wp_rows = Wp_words.rearrange("g p n t -> p g (n t)").bitcast(I32)
+        wg_rows = Wg_words.rearrange("g p n t -> p g (n t)").bitcast(I32)
+
+        v_sb = keep.tile([P, Z_PASSES, PACK, STEPS * PIXELS], BF16)
+        a_sb = keep.tile([P, 2, A_PASSES, PACK, HALF], BF16)
+        wp_codes = keep.tile([P, PASSES, D], I32, align_bytes=64)
+        wg_codes = keep.tile([P, PASSES, D], I32, align_bytes=64)
+
+        nc.scalar.dma_start(out=bp_rows[0 : D // P, :], in_=bp.rearrange("(r n) -> r n", n=P))
+        nc.scalar.dma_start(out=bg_rows[0:1, :], in_=bg.rearrange("(o n) -> o n", o=1))
+        for g in range(Z_PASSES):
+            for pair in (slice(0, 2), slice(2, 4)):
+                nc.sync.dma_start(out=v_sb[:, g, pair, :], in_=v_rows[g, :, pair, :])
+        for planes, scales in ((wp_planes, Wp_scales), (wg_planes, Wg_scales)):
+            for quad in range(4):
+                nc.sync.dma_start(
+                    out=planes[32 * quad : 32 * quad + 4, :, :].bitcast(I32),
+                    in_=scales[:, 4 * quad : 4 * quad + 4, :].rearrange("g r n -> r g n").bitcast(I32),
+                )
+        z_part = slice(A_PASSES, PASSES)
+        a_part = slice(0, A_PASSES)
+        nc.sync.dma_start(out=wp_codes[:, z_part, :], in_=wp_rows[:, z_part, :])
+        nc.sync.dma_start(out=wg_codes[:, z_part, :], in_=wg_rows[:, z_part, :])
+        for g in range(A_PASSES):
+            nc.sync.dma_start(out=a_sb[:, 0, g, :, :], in_=a_rows[g, :, :, 0:HALF])
+        nc.sync.dma_start(out=wp_codes[:, a_part, :], in_=wp_rows[:, a_part, :])
+        nc.sync.dma_start(out=wg_codes[:, a_part, :], in_=wg_rows[:, a_part, :])
+        for g in range(A_PASSES):
+            nc.sync.dma_start(out=a_sb[:, 1, g, :, :], in_=a_rows[g, :, :, HALF:COLS])
+
+        bp_bank = psum.tile([P, BANK], F32, tag="bank")
+        nc.tensor.matmul(out=bp_bank[:, 0:P], lhsT=bp_rows[:], rhs=ident[:], start=True, stop=True)
+        bp_col = keep.tile([P, D // P], F32)
+        nc.vector.tensor_copy(out=bp_col[:], in_=bp_bank[:, 0 : D // P])
+        bg_bank = psum.tile([P, BANK], F32, tag="bank")
+        nc.tensor.matmul(out=bg_bank[:], lhsT=ones[:], rhs=bg_rows[:], start=True, stop=True)
+        bg_all = keep.tile([P, D], F32)
+        nc.scalar.copy(out=bg_all[:], in_=bg_bank[:])
+
+        z_sum = keep.tile([P, Z_PASSES, STEPS, PACK], F32)
+        for g in range(Z_PASSES):
+            for j in range(PACK):
+                runs = v_sb[:, g, j, :].rearrange("p (t q r) -> p q t r", t=STEPS, r=PIXEL_RUN)
+                folded = psum.tile([P, STEPS, PIXEL_RUN], F32, tag="bank")
+                last = PIXELS // PIXEL_RUN - 1
+                for q in range(last + 1):
+                    nc.tensor.matmul(out=folded[:], lhsT=ident[:], rhs=runs[:, q], start=(q == 0), stop=(q == last))
+                nc.vector.tensor_reduce(out=z_sum[:, g, :, j], in_=folded[:], axis=mybir.AxisListType.X, op=ADD)
+
+        z_bf = keep.tile([P, Z_PASSES, STEPS, Z_COPIES, PACK], BF16, align_bytes=64)
+        for g in range(Z_PASSES):
+            nc.vector.tensor_scalar(
+                out=z_bf[:, g],
+                in0=z_sum[:, g].unsqueeze(2).to_broadcast([P, STEPS, Z_COPIES, PACK]),
+                scalar1=1.0 / PIXELS,
+                scalar2=None,
+                op0=MULT,
+            )
+        z_codes = keep.tile([P, Z_PASSES, P], I32, align_bytes=64)
+        nc.vector.quantize_mx(
+            out=z_codes[:].rearrange("p g w -> p (g w)").bitcast(FP8X4),
+            scales=z_planes[:].rearrange("p g w -> p (g w)"),
+            in_=z_bf[:].rearrange("p g t c j -> p (g t c j)"),
+        )
+
+        zp_bank = psum.tile([P, D // P, P], F32, tag="bank")
+        for i in range(D // P):
+            n_cols = slice(P * i, P * (i + 1))
+            for g in range(Z_PASSES):
+                nc.tensor.matmul_mx(
+                    out=zp_bank[:, i, :],
+                    lhsT=wp_codes[:, A_PASSES + g, n_cols].bitcast(FP8X4),
+                    lhsT_scale=wp_planes[:, A_PASSES + g, n_cols],
+                    rhs=z_codes[:, g, :].bitcast(FP8X4),
+                    rhs_scale=z_planes[:, g, :],
+                    start=(g == 0),
+                    stop=(g == Z_PASSES - 1),
+                )
+        phi_bias = keep.tile([P, D // P, STEPS], F32)
+        nc.vector.tensor_tensor(
+            out=phi_bias[:],
+            in0=zp_bank[:].rearrange("p i (t c) -> p i t c", c=Z_COPIES)[:, :, :, 0],
+            in1=bp_col[:].unsqueeze(2).to_broadcast([P, D // P, STEPS]),
+            op=ADD,
+        )
+
+        z_wide_codes = keep.tile([P, Z_PASSES, STEPS, P], I32, align_bytes=64)
+        z_wide_planes = keep.tile([P, Z_PASSES, STEPS, P], U8, align_bytes=64)
+        times = P // Z_COPIES
+        for g in range(Z_PASSES):
+            nc.vector.tensor_copy(
+                out=z_wide_codes[:, g].rearrange("p t (c w) -> p t c w", c=times),
+                in_=z_codes[:, g, :]
+                .rearrange("p (t w) -> p t w", t=STEPS)
+                .unsqueeze(2)
+                .to_broadcast([P, STEPS, times, Z_COPIES]),
+            )
+            nc.vector.tensor_copy(
+                out=z_wide_planes[:, g].bitcast(I32).rearrange("p t (c w) -> p t c w", c=times),
+                in_=z_planes[:, g, :]
+                .bitcast(I32)
+                .rearrange("p (t w) -> p t w", t=STEPS)
+                .unsqueeze(2)
+                .to_broadcast([P, STEPS, times, Z_COPIES // 4]),
+            )
+        g_bias = keep.tile([P, STEPS, D], F32)
+        for t in range(STEPS):
+            zg_bank = psum.tile([P, BANK], F32, tag="bank")
+            for g in range(Z_PASSES):
+                nc.tensor.matmul_mx(
+                    out=zg_bank[:],
+                    lhsT=z_wide_codes[:, g, t, :].bitcast(FP8X4),
+                    lhsT_scale=z_wide_planes[:, g, t, :],
+                    rhs=wg_codes[:, A_PASSES + g, :].bitcast(FP8X4),
+                    rhs_scale=wg_planes[:, A_PASSES + g, :],
+                    start=(g == 0),
+                    stop=(g == Z_PASSES - 1),
+                )
+            nc.vector.tensor_tensor(out=g_bias[:, t, :], in0=zg_bank[:], in1=bg_all[:], op=ADD)
+
+        a_codes = keep.tile([P, CHUNKS, A_PASSES, BANK], I32, align_bytes=64)
+        a_planes = keep.tile([P, CHUNKS, A_PASSES, BANK], U8, align_bytes=64)
+        for c in range(CHUNKS):
+            half, part = divmod(c, HALF // BANK)
+            cols = slice(BANK * part, BANK * (part + 1))
+            grouped = stage.tile([P, A_PASSES, BANK, PACK], BF16, align_bytes=64)
+            nc.vector.tensor_copy(out=grouped[:, 0], in_=a_sb[:, half, 0, :, cols].rearrange("p j w -> p w j"))
+            nc.scalar.copy(out=grouped[:, 1], in_=a_sb[:, half, 1, :, cols].rearrange("p j w -> p w j"))
+            nc.vector.quantize_mx(
+                out=a_codes[:, c].rearrange("p g w -> p (g w)").bitcast(FP8X4),
+                scales=a_planes[:, c].rearrange("p g w -> p (g w)"),
+                in_=grouped[:].rearrange("p g w j -> p (g w j)"),
+            )
+            for i in range(BANK // P):
+                block = slice(P * i, P * (i + 1))
+                phi_bank = psum.tile([P, BANK], F32, tag="bank")
+                for g in range(A_PASSES):
+                    nc.tensor.matmul_mx(
+                        out=phi_bank[:],
+                        lhsT=wp_codes[:, g, block].bitcast(FP8X4),
+                        lhsT_scale=wp_planes[:, g, block],
+                        rhs=a_codes[:, c, g, :].bitcast(FP8X4),
+                        rhs_scale=a_planes[:, c, g, :],
+                        start=(g == 0),
+                        stop=(g == A_PASSES - 1),
+                    )
+                phi_sb = results.tile([P, BANK], F32)
+                for s in range(BANK // COLS_PER_STEP):
+                    t = c * (BANK // COLS_PER_STEP) + s
+                    step_cols = slice(COLS_PER_STEP * s, COLS_PER_STEP * (s + 1))
+                    nc.scalar.activation(
+                        out=phi_sb[:, step_cols], in_=phi_bank[:, step_cols], func=IDENTITY, bias=phi_bias[:, i, t : t + 1]
+                    )
+                nc.sync.dma_start(out=out_0[0, block, BANK * c : BANK * (c + 1)], in_=phi_sb[:])
+
+                g_bank = psum.tile([P, BANK], F32, tag="bank")
+                for g in range(A_PASSES):
+                    nc.tensor.matmul_mx(
+                        out=g_bank[:],
+                        lhsT=a_codes[:, c, g, block].bitcast(FP8X4),
+                        lhsT_scale=a_planes[:, c, g, block],
+                        rhs=wg_codes[:, g, :].bitcast(FP8X4),
+                        rhs_scale=wg_planes[:, g, :],
+                        start=(g == 0),
+                        stop=(g == A_PASSES - 1),
+                    )
+                first_col = BANK * c + P * i
+                g_sb = results.tile([P, D], F32)
+                nc.vector.tensor_tensor(out=g_sb[:], in0=g_bank[:], in1=g_bias[:, first_col // COLS_PER_STEP, :], op=ADD)
+                nc.sync.dma_start(out=out_1[0, first_col : first_col + P, :], in_=g_sb[:])

@@ -26,6 +26,7 @@ BANK = 512
 HALF = COLS // 2
 CHUNKS = COLS // BANK
 PIXEL_RUN = BANK // STEPS
+N_TILES = D // P
 Z_COPIES = P // STEPS
 
 FLOPS = 2 * 2 * D * COLS * (PASSES * P * PACK)
@@ -35,24 +36,21 @@ def tile_nlgate_pa_kernel(tc, v, a, Wp_words, Wp_scales, bp, Wg_words, Wg_scales
     nc = tc.nc
     with ExitStack() as ctx:
         keep = ctx.enter_context(tc.tile_pool(name="keep", bufs=1))
-        stage = ctx.enter_context(tc.tile_pool(name="stage", bufs=2))
-        results = ctx.enter_context(tc.tile_pool(name="results", bufs=4))
+        stage = ctx.enter_context(tc.tile_pool(name="stage", bufs=4))
+        results = ctx.enter_context(tc.tile_pool(name="results", bufs=6))
         psum = ctx.enter_context(tc.psum_pool(name="psum", bufs=8))
+        ctx.enter_context(tc.manual_schedule())
 
         ident = keep.tile([P, P], BF16)
         make_identity(nc, ident[:])
-        ones = keep.tile([P, P], BF16)
-        nc.vector.memset(ones[:], 1.0)
-        bp_rows = keep.tile([P, P], BF16)
-        nc.vector.memset(bp_rows[:], 0.0)
-        bg_rows = keep.tile([P, D], BF16)
-        nc.vector.memset(bg_rows[:], 0.0)
+        ident_f32 = keep.tile([P, P], F32)
+        make_identity(nc, ident_f32[:])
+        bias_rows = keep.tile([P, P], BF16)
+        nc.vector.memset(bias_rows[:], 0.0)
         wp_planes = keep.tile([P, PASSES, D], U8, align_bytes=64)
         wg_planes = keep.tile([P, PASSES, D], U8, align_bytes=64)
         nc.vector.memset(wp_planes[:].bitcast(I32), 0)
         nc.vector.memset(wg_planes[:].bitcast(I32), 0)
-        z_planes = keep.tile([P, Z_PASSES, P], U8, align_bytes=64)
-        nc.vector.memset(z_planes[:].bitcast(I32), 0)
 
         v_rows = v[0].rearrange("(g p j) t h w -> g p j (t h w)", p=P, j=PACK)
         a_rows = a[0].rearrange("(g p j) i f -> g p j (i f)", p=P, j=PACK)
@@ -64,11 +62,11 @@ def tile_nlgate_pa_kernel(tc, v, a, Wp_words, Wp_scales, bp, Wg_words, Wg_scales
         wp_codes = keep.tile([P, PASSES, D], I32, align_bytes=64)
         wg_codes = keep.tile([P, PASSES, D], I32, align_bytes=64)
 
-        nc.scalar.dma_start(out=bp_rows[0 : D // P, :], in_=bp.rearrange("(r n) -> r n", n=P))
-        nc.scalar.dma_start(out=bg_rows[0:1, :], in_=bg.rearrange("(o n) -> o n", o=1))
+        nc.scalar.dma_start(out=bias_rows[0:N_TILES, :], in_=bp.rearrange("(r n) -> r n", n=P))
+        nc.scalar.dma_start(out=bias_rows[N_TILES : 2 * N_TILES, :], in_=bg.rearrange("(r n) -> r n", n=P))
         for g in range(Z_PASSES):
-            for pair in (slice(0, 2), slice(2, 4)):
-                nc.sync.dma_start(out=v_sb[:, g, pair, :], in_=v_rows[g, :, pair, :])
+            for j in range(PACK):
+                nc.sync.dma_start(out=v_sb[:, g, j, :], in_=v_rows[g, :, j, :])
         for planes, scales in ((wp_planes, Wp_scales), (wg_planes, Wg_scales)):
             for quad in range(4):
                 nc.sync.dma_start(
@@ -79,150 +77,152 @@ def tile_nlgate_pa_kernel(tc, v, a, Wp_words, Wp_scales, bp, Wg_words, Wg_scales
         a_part = slice(0, A_PASSES)
         nc.sync.dma_start(out=wp_codes[:, z_part, :], in_=wp_rows[:, z_part, :])
         nc.sync.dma_start(out=wg_codes[:, z_part, :], in_=wg_rows[:, z_part, :])
-        for g in range(A_PASSES):
+        for g in reversed(range(A_PASSES)):
             nc.sync.dma_start(out=a_sb[:, 0, g, :, :], in_=a_rows[g, :, :, 0:HALF])
         nc.sync.dma_start(out=wp_codes[:, a_part, :], in_=wp_rows[:, a_part, :])
         nc.sync.dma_start(out=wg_codes[:, a_part, :], in_=wg_rows[:, a_part, :])
-        for g in range(A_PASSES):
+        for g in reversed(range(A_PASSES)):
             nc.sync.dma_start(out=a_sb[:, 1, g, :, :], in_=a_rows[g, :, :, HALF:COLS])
 
-        bp_bank = psum.tile([P, BANK], F32, tag="bank")
-        nc.tensor.matmul(out=bp_bank[:, 0:P], lhsT=bp_rows[:], rhs=ident[:], start=True, stop=True)
-        bp_col = keep.tile([P, D // P], F32)
-        nc.vector.tensor_copy(out=bp_col[:], in_=bp_bank[:, 0 : D // P])
-        bg_bank = psum.tile([P, BANK], F32, tag="bank")
-        nc.tensor.matmul(out=bg_bank[:], lhsT=ones[:], rhs=bg_rows[:], start=True, stop=True)
-        bg_all = keep.tile([P, D], F32)
-        nc.scalar.copy(out=bg_all[:], in_=bg_bank[:])
-
-        z_sum = keep.tile([P, Z_PASSES, STEPS, PACK], F32)
+        z_sum = keep.tile([P, Z_PASSES, PACK, STEPS], F32)
+        z_bf = keep.tile([P, Z_PASSES, STEPS, Z_COPIES, PACK], BF16, align_bytes=64)
+        z_codes = keep.tile([P, Z_PASSES, P], I32, align_bytes=64)
+        z_planes = keep.tile([P, Z_PASSES, P], U8, align_bytes=64)
+        unused = keep.tile([P, PIXELS], BF16)
         for g in range(Z_PASSES):
-            for j in range(PACK):
+            for t in range(STEPS):
+                nc.scalar.activation(
+                    out=unused[:],
+                    in_=v_sb[:, g, 0, PIXELS * t : PIXELS * (t + 1)],
+                    func=IDENTITY,
+                    accum_out=z_sum[:, g, 0, t : t + 1],
+                )
+            for j in range(1, PACK):
                 runs = v_sb[:, g, j, :].rearrange("p (t q r) -> p q t r", t=STEPS, r=PIXEL_RUN)
                 folded = psum.tile([P, STEPS, PIXEL_RUN], F32, tag="bank")
                 last = PIXELS // PIXEL_RUN - 1
                 for q in range(last + 1):
                     nc.tensor.matmul(out=folded[:], lhsT=ident[:], rhs=runs[:, q], start=(q == 0), stop=(q == last))
-                nc.vector.tensor_reduce(out=z_sum[:, g, :, j], in_=folded[:], axis=mybir.AxisListType.X, op=ADD)
-
-        z_bf = keep.tile([P, Z_PASSES, STEPS, Z_COPIES, PACK], BF16, align_bytes=64)
-        for g in range(Z_PASSES):
+                nc.vector.tensor_reduce(out=z_sum[:, g, j, :], in_=folded[:], axis=mybir.AxisListType.X, op=ADD)
             nc.vector.tensor_scalar(
                 out=z_bf[:, g],
-                in0=z_sum[:, g].unsqueeze(2).to_broadcast([P, STEPS, Z_COPIES, PACK]),
+                in0=z_sum[:, g].rearrange("p j t -> p t j").unsqueeze(2).to_broadcast([P, STEPS, Z_COPIES, PACK]),
                 scalar1=1.0 / PIXELS,
                 scalar2=None,
                 op0=MULT,
             )
-        z_codes = keep.tile([P, Z_PASSES, P], I32, align_bytes=64)
-        nc.vector.quantize_mx(
-            out=z_codes[:].rearrange("p g w -> p (g w)").bitcast(FP8X4),
-            scales=z_planes[:].rearrange("p g w -> p (g w)"),
-            in_=z_bf[:].rearrange("p g t c j -> p (g t c j)"),
-        )
-
-        zp_bank = psum.tile([P, D // P, P], F32, tag="bank")
-        for i in range(D // P):
-            n_cols = slice(P * i, P * (i + 1))
-            for g in range(Z_PASSES):
-                nc.tensor.matmul_mx(
-                    out=zp_bank[:, i, :],
-                    lhsT=wp_codes[:, A_PASSES + g, n_cols].bitcast(FP8X4),
-                    lhsT_scale=wp_planes[:, A_PASSES + g, n_cols],
-                    rhs=z_codes[:, g, :].bitcast(FP8X4),
-                    rhs_scale=z_planes[:, g, :],
-                    start=(g == 0),
-                    stop=(g == Z_PASSES - 1),
-                )
-        phi_bias = keep.tile([P, D // P, STEPS], F32)
-        nc.vector.tensor_tensor(
-            out=phi_bias[:],
-            in0=zp_bank[:].rearrange("p i (t c) -> p i t c", c=Z_COPIES)[:, :, :, 0],
-            in1=bp_col[:].unsqueeze(2).to_broadcast([P, D // P, STEPS]),
-            op=ADD,
-        )
-
-        z_wide_codes = keep.tile([P, Z_PASSES, STEPS, P], I32, align_bytes=64)
-        z_wide_planes = keep.tile([P, Z_PASSES, STEPS, P], U8, align_bytes=64)
-        times = P // Z_COPIES
-        for g in range(Z_PASSES):
-            nc.vector.tensor_copy(
-                out=z_wide_codes[:, g].rearrange("p t (c w) -> p t c w", c=times),
-                in_=z_codes[:, g, :]
-                .rearrange("p (t w) -> p t w", t=STEPS)
-                .unsqueeze(2)
-                .to_broadcast([P, STEPS, times, Z_COPIES]),
+            nc.vector.quantize_mx(
+                out=z_codes[:, g, :].bitcast(FP8X4),
+                scales=z_planes[:, g, :],
+                in_=z_bf[:, g].rearrange("p t c j -> p (t c j)"),
             )
-            nc.vector.tensor_copy(
-                out=z_wide_planes[:, g].bitcast(I32).rearrange("p t (c w) -> p t c w", c=times),
-                in_=z_planes[:, g, :]
-                .bitcast(I32)
-                .rearrange("p (t w) -> p t w", t=STEPS)
-                .unsqueeze(2)
-                .to_broadcast([P, STEPS, times, Z_COPIES // 4]),
-            )
-        g_bias = keep.tile([P, STEPS, D], F32)
-        for t in range(STEPS):
-            zg_bank = psum.tile([P, BANK], F32, tag="bank")
-            for g in range(Z_PASSES):
-                nc.tensor.matmul_mx(
-                    out=zg_bank[:],
-                    lhsT=z_wide_codes[:, g, t, :].bitcast(FP8X4),
-                    lhsT_scale=z_wide_planes[:, g, t, :],
-                    rhs=wg_codes[:, A_PASSES + g, :].bitcast(FP8X4),
-                    rhs_scale=wg_planes[:, A_PASSES + g, :],
-                    start=(g == 0),
-                    stop=(g == Z_PASSES - 1),
-                )
-            nc.vector.tensor_tensor(out=g_bias[:, t, :], in0=zg_bank[:], in1=bg_all[:], op=ADD)
 
         a_codes = keep.tile([P, CHUNKS, A_PASSES, BANK], I32, align_bytes=64)
         a_planes = keep.tile([P, CHUNKS, A_PASSES, BANK], U8, align_bytes=64)
-        for c in range(CHUNKS):
-            half, part = divmod(c, HALF // BANK)
-            cols = slice(BANK * part, BANK * (part + 1))
-            grouped = stage.tile([P, A_PASSES, BANK, PACK], BF16, align_bytes=64)
-            nc.vector.tensor_copy(out=grouped[:, 0], in_=a_sb[:, half, 0, :, cols].rearrange("p j w -> p w j"))
-            nc.scalar.copy(out=grouped[:, 1], in_=a_sb[:, half, 1, :, cols].rearrange("p j w -> p w j"))
-            nc.vector.quantize_mx(
-                out=a_codes[:, c].rearrange("p g w -> p (g w)").bitcast(FP8X4),
-                scales=a_planes[:, c].rearrange("p g w -> p (g w)"),
-                in_=grouped[:].rearrange("p g w j -> p (g w j)"),
-            )
-            for i in range(BANK // P):
-                block = slice(P * i, P * (i + 1))
-                phi_bank = psum.tile([P, BANK], F32, tag="bank")
-                for g in range(A_PASSES):
-                    nc.tensor.matmul_mx(
-                        out=phi_bank[:],
-                        lhsT=wp_codes[:, g, block].bitcast(FP8X4),
-                        lhsT_scale=wp_planes[:, g, block],
-                        rhs=a_codes[:, c, g, :].bitcast(FP8X4),
-                        rhs_scale=a_planes[:, c, g, :],
-                        start=(g == 0),
-                        stop=(g == A_PASSES - 1),
-                    )
-                phi_sb = results.tile([P, BANK], F32)
-                for s in range(BANK // COLS_PER_STEP):
-                    t = c * (BANK // COLS_PER_STEP) + s
-                    step_cols = slice(COLS_PER_STEP * s, COLS_PER_STEP * (s + 1))
-                    nc.scalar.activation(
-                        out=phi_sb[:, step_cols], in_=phi_bank[:, step_cols], func=IDENTITY, bias=phi_bias[:, i, t : t + 1]
-                    )
-                nc.sync.dma_start(out=out_0[0, block, BANK * c : BANK * (c + 1)], in_=phi_sb[:])
 
-                g_bank = psum.tile([P, BANK], F32, tag="bank")
-                for g in range(A_PASSES):
+        def regroup(c, g):
+            half, part = divmod(c, HALF // BANK)
+            rows = a_sb[:, half, g, :, BANK * part : BANK * (part + 1)]
+            grouped = stage.tile([P, BANK, PACK], BF16, align_bytes=64)
+            copy = nc.vector.tensor_copy if g == 0 else nc.scalar.copy
+            copy(out=grouped[:], in_=rows.rearrange("p j w -> p w j"))
+            return grouped
+
+        def quantise(c, g, grouped):
+            nc.vector.quantize_mx(
+                out=a_codes[:, c, g, :].bitcast(FP8X4),
+                scales=a_planes[:, c, g, :],
+                in_=grouped[:].rearrange("p w j -> p (w j)"),
+            )
+
+        def phi_tile(c, i):
+            block = slice(P * i, P * (i + 1))
+            phi_bank = psum.tile([P, BANK], F32, tag="bank")
+            for g in range(A_PASSES):
+                nc.tensor.matmul_mx(
+                    out=phi_bank[:],
+                    lhsT=wp_codes[:, g, block].bitcast(FP8X4),
+                    lhsT_scale=wp_planes[:, g, block],
+                    rhs=a_codes[:, c, g, :].bitcast(FP8X4),
+                    rhs_scale=a_planes[:, c, g, :],
+                    start=(g == 0),
+                    stop=(g == A_PASSES - 1),
+                )
+            phi_sb = results.tile([P, BANK], F32)
+            for s in range(BANK // COLS_PER_STEP):
+                t = c * (BANK // COLS_PER_STEP) + s
+                step_cols = slice(COLS_PER_STEP * s, COLS_PER_STEP * (s + 1))
+                nc.scalar.activation(
+                    out=phi_sb[:, step_cols], in_=phi_bank[:, step_cols], func=IDENTITY, bias=step_bias[:, 0, i, t : t + 1]
+                )
+            nc.sync.dma_start(out=out_0[0, block, BANK * c : BANK * (c + 1)], in_=phi_sb[:])
+
+        def g_tile(c, i):
+            block = slice(P * i, P * (i + 1))
+            g_bank = psum.tile([P, BANK], F32, tag="bank")
+            for g in range(A_PASSES):
+                nc.tensor.matmul_mx(
+                    out=g_bank[:],
+                    lhsT=a_codes[:, c, g, block].bitcast(FP8X4),
+                    lhsT_scale=a_planes[:, c, g, block],
+                    rhs=wg_codes[:, g, :].bitcast(FP8X4),
+                    rhs_scale=wg_planes[:, g, :],
+                    start=(g == 0),
+                    stop=(g == A_PASSES - 1),
+                )
+            first_col = BANK * c + P * i
+            g_sb = results.tile([P, D], F32)
+            nc.vector.tensor_tensor(out=g_sb[:], in0=g_bank[:], in1=g_bias[:, first_col // COLS_PER_STEP, :], op=ADD)
+            nc.sync.dma_start(out=out_1[0, first_col : first_col + P, :], in_=g_sb[:])
+
+        bias_bank = psum.tile([P, BANK], F32, tag="bank")
+        nc.tensor.matmul(out=bias_bank[:, 0:P], lhsT=bias_rows[:], rhs=ident[:], start=True, stop=True)
+        bias_col = keep.tile([P, 2, N_TILES], F32)
+        nc.vector.tensor_copy(out=bias_col[:].rearrange("p b i -> p (b i)"), in_=bias_bank[:, 0 : 2 * N_TILES])
+        step_bias = keep.tile([P, 2, N_TILES, STEPS], F32)
+        for b, codes, planes in ((0, wp_codes, wp_planes), (1, wg_codes, wg_planes)):
+            z_bank = psum.tile([P, N_TILES, P], F32, tag="bank")
+            for i in range(N_TILES):
+                n_cols = slice(P * i, P * (i + 1))
+                for g in range(Z_PASSES):
                     nc.tensor.matmul_mx(
-                        out=g_bank[:],
-                        lhsT=a_codes[:, c, g, block].bitcast(FP8X4),
-                        lhsT_scale=a_planes[:, c, g, block],
-                        rhs=wg_codes[:, g, :].bitcast(FP8X4),
-                        rhs_scale=wg_planes[:, g, :],
+                        out=z_bank[:, i, :],
+                        lhsT=codes[:, A_PASSES + g, n_cols].bitcast(FP8X4),
+                        lhsT_scale=planes[:, A_PASSES + g, n_cols],
+                        rhs=z_codes[:, g, :].bitcast(FP8X4),
+                        rhs_scale=z_planes[:, g, :],
                         start=(g == 0),
-                        stop=(g == A_PASSES - 1),
+                        stop=(g == Z_PASSES - 1),
                     )
-                first_col = BANK * c + P * i
-                g_sb = results.tile([P, D], F32)
-                nc.vector.tensor_tensor(out=g_sb[:], in0=g_bank[:], in1=g_bias[:, first_col // COLS_PER_STEP, :], op=ADD)
-                nc.sync.dma_start(out=out_1[0, first_col : first_col + P, :], in_=g_sb[:])
+            nc.vector.tensor_tensor(
+                out=step_bias[:, b],
+                in0=z_bank[:].rearrange("p i (t c) -> p i t c", c=Z_COPIES)[:, :, :, 0],
+                in1=bias_col[:, b, :].unsqueeze(2).to_broadcast([P, N_TILES, STEPS]),
+                op=ADD,
+            )
+        grouped = {1: regroup(0, 1)}
+        g_bias = keep.tile([P, STEPS, D], F32)
+        for t in range(STEPS):
+            spread = psum.tile([P, BANK], F32, tag="bank")
+            for i in range(N_TILES):
+                nc.tensor.transpose(
+                    spread[:, P * i : P * (i + 1)], step_bias[:, 1, i, t : t + 1].to_broadcast([P, P]), ident_f32[:]
+                )
+            if t % 2 == 0:
+                nc.vector.tensor_copy(out=g_bias[:, t, :], in_=spread[:])
+            else:
+                nc.scalar.copy(out=g_bias[:, t, :], in_=spread[:])
+
+        grouped[0] = regroup(0, 0)
+        for g in range(A_PASSES):
+            quantise(0, g, grouped[g])
+        for c in range(CHUNKS):
+            more = c + 1 < CHUNKS
+            if more:
+                grouped = {g: regroup(c + 1, g) for g in range(A_PASSES)}
+            for i in range(N_TILES):
+                if more and i == N_TILES // 2:
+                    for g in range(A_PASSES):
+                        quantise(c + 1, g, grouped[g])
+                phi_tile(c, i)
+                g_tile(c, i)

@@ -46,11 +46,11 @@ def tile_nlgate_pa_kernel(tc, v, a, Wp_words, Wp_scales, bp, Wg_words, Wg_scales
         ident_f32 = keep.tile([P, P], F32)
         make_identity(nc, ident_f32[:])
         bias_rows = keep.tile([P, P], BF16)
-        nc.vector.memset(bias_rows[:], 0.0)
         wp_planes = keep.tile([P, PASSES, D], U8, align_bytes=64)
         wg_planes = keep.tile([P, PASSES, D], U8, align_bytes=64)
-        nc.vector.memset(wp_planes[:].bitcast(I32), 0)
         nc.vector.memset(wg_planes[:].bitcast(I32), 0)
+        nc.vector.memset(bias_rows[:], 0.0)
+        nc.vector.memset(wp_planes[:].bitcast(I32), 0)
 
         v_rows = v[0].rearrange("(g p j) t h w -> g p j (t h w)", p=P, j=PACK)
         a_rows = a[0].rearrange("(g p j) i f -> g p j (i f)", p=P, j=PACK)
@@ -64,25 +64,31 @@ def tile_nlgate_pa_kernel(tc, v, a, Wp_words, Wp_scales, bp, Wg_words, Wg_scales
 
         nc.scalar.dma_start(out=bias_rows[0:N_TILES, :], in_=bp.rearrange("(r n) -> r n", n=P))
         nc.scalar.dma_start(out=bias_rows[N_TILES : 2 * N_TILES, :], in_=bg.rearrange("(r n) -> r n", n=P))
-        for g in range(Z_PASSES):
-            for j in range(PACK):
-                nc.sync.dma_start(out=v_sb[:, g, j, :], in_=v_rows[g, :, j, :])
-        for planes, scales in ((wp_planes, Wp_scales), (wg_planes, Wg_scales)):
+        def load_planes(planes, scales):
             for quad in range(4):
                 nc.sync.dma_start(
                     out=planes[32 * quad : 32 * quad + 4, :, :].bitcast(I32),
                     in_=scales[:, 4 * quad : 4 * quad + 4, :].rearrange("g r n -> r g n").bitcast(I32),
                 )
+
+        def load_a(half):
+            for g in reversed(range(A_PASSES)):
+                nc.sync.dma_start(out=a_sb[:, half, g, :, :], in_=a_rows[g, :, :, HALF * half : HALF * (half + 1)])
+
         z_part = slice(A_PASSES, PASSES)
         a_part = slice(0, A_PASSES)
-        nc.sync.dma_start(out=wp_codes[:, z_part, :], in_=wp_rows[:, z_part, :])
+        for g in range(Z_PASSES):
+            for j in range(PACK):
+                if (g, j) == (0, 2):
+                    load_planes(wg_planes, Wg_scales)
+                nc.sync.dma_start(out=v_sb[:, g, j, :], in_=v_rows[g, :, j, :])
         nc.sync.dma_start(out=wg_codes[:, z_part, :], in_=wg_rows[:, z_part, :])
-        for g in reversed(range(A_PASSES)):
-            nc.sync.dma_start(out=a_sb[:, 0, g, :, :], in_=a_rows[g, :, :, 0:HALF])
+        load_a(0)
+        load_planes(wp_planes, Wp_scales)
+        nc.sync.dma_start(out=wp_codes[:, z_part, :], in_=wp_rows[:, z_part, :])
         nc.sync.dma_start(out=wp_codes[:, a_part, :], in_=wp_rows[:, a_part, :])
         nc.sync.dma_start(out=wg_codes[:, a_part, :], in_=wg_rows[:, a_part, :])
-        for g in reversed(range(A_PASSES)):
-            nc.sync.dma_start(out=a_sb[:, 1, g, :, :], in_=a_rows[g, :, :, HALF:COLS])
+        load_a(1)
 
         z_sum = keep.tile([P, Z_PASSES, PACK, STEPS], F32)
         z_bf = keep.tile([P, Z_PASSES, STEPS, Z_COPIES, PACK], BF16, align_bytes=64)
@@ -180,7 +186,8 @@ def tile_nlgate_pa_kernel(tc, v, a, Wp_words, Wp_scales, bp, Wg_words, Wg_scales
         bias_col = keep.tile([P, 2, N_TILES], F32)
         nc.vector.tensor_copy(out=bias_col[:].rearrange("p b i -> p (b i)"), in_=bias_bank[:, 0 : 2 * N_TILES])
         step_bias = keep.tile([P, 2, N_TILES, STEPS], F32)
-        for b, codes, planes in ((0, wp_codes, wp_planes), (1, wg_codes, wg_planes)):
+
+        def video_share(b, codes, planes):
             z_bank = psum.tile([P, N_TILES, P], F32, tag="bank")
             for i in range(N_TILES):
                 n_cols = slice(P * i, P * (i + 1))
@@ -200,22 +207,28 @@ def tile_nlgate_pa_kernel(tc, v, a, Wp_words, Wp_scales, bp, Wg_words, Wg_scales
                 in1=bias_col[:, b, :].unsqueeze(2).to_broadcast([P, N_TILES, STEPS]),
                 op=ADD,
             )
+        video_share(1, wg_codes, wg_planes)
         grouped = {1: regroup(0, 1)}
         g_bias = keep.tile([P, STEPS, D], F32)
+        spreads = []
         for t in range(STEPS):
             spread = psum.tile([P, BANK], F32, tag="bank")
+            spreads.append(spread)
             for i in range(N_TILES):
                 nc.tensor.transpose(
                     spread[:, P * i : P * (i + 1)], step_bias[:, 1, i, t : t + 1].to_broadcast([P, P]), ident_f32[:]
                 )
-            if t % 2 == 0:
-                nc.vector.tensor_copy(out=g_bias[:, t, :], in_=spread[:])
-            else:
+            if t % 2 == 1:
                 nc.scalar.copy(out=g_bias[:, t, :], in_=spread[:])
+            elif t < STEPS // 2:
+                nc.vector.tensor_copy(out=g_bias[:, t, :], in_=spread[:])
 
         grouped[0] = regroup(0, 0)
-        for g in range(A_PASSES):
+        for g in reversed(range(A_PASSES)):
             quantise(0, g, grouped[g])
+        video_share(0, wp_codes, wp_planes)
+        for t in range(STEPS // 2, STEPS, 2):
+            nc.vector.tensor_copy(out=g_bias[:, t, :], in_=spreads[t][:])
         for c in range(CHUNKS):
             more = c + 1 < CHUNKS
             if more:

@@ -46,8 +46,8 @@ def tile_nlgate_pa_kernel(tc, v, a, Wp_words, Wp_scales, bp, Wg_words, Wg_scales
         ident_f32 = keep.tile([P, P], F32)
         make_identity(nc, ident_f32[:])
         bias_rows = keep.tile([P, P], BF16)
-        wp_planes = keep.tile([P, PASSES, D], U8, align_bytes=64)
-        wg_planes = keep.tile([P, PASSES, D], U8, align_bytes=64)
+        wp_planes = keep.tile([P, D], U8, align_bytes=64)
+        wg_planes = keep.tile([P, D], U8, align_bytes=64)
         nc.vector.memset(wg_planes[:].bitcast(I32), 0)
         nc.vector.memset(bias_rows[:], 0.0)
         nc.vector.memset(wp_planes[:].bitcast(I32), 0)
@@ -67,8 +67,8 @@ def tile_nlgate_pa_kernel(tc, v, a, Wp_words, Wp_scales, bp, Wg_words, Wg_scales
         def load_planes(planes, scales):
             for quad in range(4):
                 nc.sync.dma_start(
-                    out=planes[32 * quad : 32 * quad + 4, :, :].bitcast(I32),
-                    in_=scales[:, 4 * quad : 4 * quad + 4, :].rearrange("g r n -> r g n").bitcast(I32),
+                    out=planes[32 * quad : 32 * quad + 4 * PASSES, :].bitcast(I32),
+                    in_=scales[:, 4 * quad : 4 * quad + 4, :].bitcast(I32),
                 )
 
         def load_a(half):
@@ -148,7 +148,7 @@ def tile_nlgate_pa_kernel(tc, v, a, Wp_words, Wp_scales, bp, Wg_words, Wg_scales
                 nc.tensor.matmul_mx(
                     out=phi_bank[:],
                     lhsT=wp_codes[:, g, block].bitcast(FP8X4),
-                    lhsT_scale=wp_planes[:, g, block],
+                    lhsT_scale=wp_planes[4 * g : P, block],
                     rhs=a_codes[:, c, g, :].bitcast(FP8X4),
                     rhs_scale=a_planes[:, c, g, :],
                     start=(g == 0),
@@ -172,7 +172,7 @@ def tile_nlgate_pa_kernel(tc, v, a, Wp_words, Wp_scales, bp, Wg_words, Wg_scales
                     lhsT=a_codes[:, c, g, block].bitcast(FP8X4),
                     lhsT_scale=a_planes[:, c, g, block],
                     rhs=wg_codes[:, g, :].bitcast(FP8X4),
-                    rhs_scale=wg_planes[:, g, :],
+                    rhs_scale=wg_planes[4 * g : P, :],
                     start=(g == 0),
                     stop=(g == A_PASSES - 1),
                 )
@@ -195,7 +195,7 @@ def tile_nlgate_pa_kernel(tc, v, a, Wp_words, Wp_scales, bp, Wg_words, Wg_scales
                     nc.tensor.matmul_mx(
                         out=z_bank[:, i, :],
                         lhsT=codes[:, A_PASSES + g, n_cols].bitcast(FP8X4),
-                        lhsT_scale=planes[:, A_PASSES + g, n_cols],
+                        lhsT_scale=planes[4 * (A_PASSES + g) : P, n_cols],
                         rhs=z_codes[:, g, :].bitcast(FP8X4),
                         rhs_scale=z_planes[:, g, :],
                         start=(g == 0),

@@ -28,6 +28,9 @@ CHUNKS = COLS // BANK
 PIXEL_RUN = BANK // STEPS
 N_TILES = D // P
 Z_COPIES = P // STEPS
+STEPS_PER_CHUNK = BANK // COLS_PER_STEP
+HANDS = 2
+HAND_COLS = BANK // HANDS
 
 FLOPS = 2 * 2 * D * COLS * (PASSES * P * PACK)
 
@@ -36,7 +39,8 @@ def tile_nlgate_pa_kernel(tc, v, a, Wp_words, Wp_scales, bp, Wg_words, Wg_scales
     nc = tc.nc
     with ExitStack() as ctx:
         keep = ctx.enter_context(tc.tile_pool(name="keep", bufs=1))
-        stage = ctx.enter_context(tc.tile_pool(name="stage", bufs=4))
+        stage = ctx.enter_context(tc.tile_pool(name="stage", bufs=2))
+        stage_0 = ctx.enter_context(tc.tile_pool(name="stage_0", bufs=1))
         results = ctx.enter_context(tc.tile_pool(name="results", bufs=6))
         psum = ctx.enter_context(tc.psum_pool(name="psum", bufs=8))
         ctx.enter_context(tc.manual_schedule())
@@ -128,11 +132,18 @@ def tile_nlgate_pa_kernel(tc, v, a, Wp_words, Wp_scales, bp, Wg_words, Wg_scales
 
         def regroup(c, g):
             half, part = divmod(c, HALF // BANK)
-            rows = a_sb[:, half, g, :, BANK * part : BANK * (part + 1)]
-            grouped = stage.tile([P, BANK, PACK], BF16, align_bytes=64)
-            copy = nc.vector.tensor_copy if g == 0 else nc.scalar.copy
-            copy(out=grouped[:], in_=rows.rearrange("p j w -> p w j"))
-            return grouped
+            rows = a_sb[:, half, g, :, BANK * part : BANK * (part + 1)].rearrange("p j (m s) -> p s m j", s=HANDS)
+            if g == 1:
+                grouped = stage.tile([P, BANK, PACK], BF16, align_bytes=64)
+                nc.scalar.copy(out=grouped[:].rearrange("p (s m) j -> p s m j", s=HANDS), in_=rows)
+                return grouped
+            grouped_0 = stage_0.tile([P, BANK, PACK], BF16, align_bytes=64)
+            dealt = grouped_0[:].rearrange("p (s m) j -> p s m j", s=HANDS)
+            if c == 0:
+                nc.vector.tensor_copy(out=dealt, in_=rows)
+            else:
+                nc.gpsimd.tensor_scalar(out=dealt, in0=rows, scalar1=1.0, scalar2=0.0, op0=MULT, op1=ADD)
+            return grouped_0
 
         def quantise(c, g, grouped):
             nc.vector.quantize_mx(
@@ -140,6 +151,8 @@ def tile_nlgate_pa_kernel(tc, v, a, Wp_words, Wp_scales, bp, Wg_words, Wg_scales
                 scales=a_planes[:, c, g, :],
                 in_=grouped[:].rearrange("p w j -> p (w j)"),
             )
+
+        pairs = {}
 
         def phi_tile(c, i):
             block = slice(P * i, P * (i + 1))
@@ -154,17 +167,37 @@ def tile_nlgate_pa_kernel(tc, v, a, Wp_words, Wp_scales, bp, Wg_words, Wg_scales
                     start=(g == 0),
                     stop=(g == A_PASSES - 1),
                 )
-            phi_sb = results.tile([P, BANK], F32)
-            for s in range(BANK // COLS_PER_STEP):
-                t = c * (BANK // COLS_PER_STEP) + s
-                step_cols = slice(COLS_PER_STEP * s, COLS_PER_STEP * (s + 1))
-                nc.scalar.activation(
-                    out=phi_sb[:, step_cols], in_=phi_bank[:, step_cols], func=IDENTITY, bias=step_bias[:, 0, i, t : t + 1]
+            k, second = divmod(i, 2)
+            if second == 0:
+                phi_sb = results.tile([P, 2, BANK], F32)
+                pairs[0] = phi_sb
+            phi_sb = pairs[0]
+            first_step = c * STEPS_PER_CHUNK
+            by_step = phi_bank[:].rearrange("p (s u m) -> p u m s", s=HANDS, u=STEPS_PER_CHUNK)
+            in_order = phi_sb[:, second, :].rearrange("p (u m s) -> p u m s", u=STEPS_PER_CHUNK, s=HANDS)
+            if i == N_TILES - 1:
+                nc.vector.tensor_tensor(
+                    out=in_order,
+                    in0=by_step,
+                    in1=step_bias[:, 0, i, first_step : first_step + STEPS_PER_CHUNK]
+                    .unsqueeze(2)
+                    .unsqueeze(3)
+                    .to_broadcast([P, STEPS_PER_CHUNK, P, HANDS]),
+                    op=ADD,
                 )
-            nc.sync.dma_start(out=out_0[0, block, BANK * c : BANK * (c + 1)], in_=phi_sb[:])
+            else:
+                for u in range(STEPS_PER_CHUNK):
+                    t = first_step + u
+                    nc.scalar.activation(
+                        out=in_order[:, u], in_=by_step[:, u], func=IDENTITY, bias=step_bias[:, 0, i, t : t + 1]
+                    )
+            if second == 1:
+                two_blocks = out_0[0, 2 * P * k : 2 * P * (k + 1), BANK * c : BANK * (c + 1)]
+                nc.sync.dma_start(out=two_blocks.rearrange("(i p) w -> p i w", p=P), in_=phi_sb[:])
 
         def g_tile(c, i):
-            block = slice(P * i, P * (i + 1))
+            u, s = divmod(i, HANDS)
+            block = slice(HAND_COLS * s + P * u, HAND_COLS * s + P * (u + 1))
             g_bank = psum.tile([P, BANK], F32, tag="bank")
             for g in range(A_PASSES):
                 nc.tensor.matmul_mx(
@@ -176,10 +209,17 @@ def tile_nlgate_pa_kernel(tc, v, a, Wp_words, Wp_scales, bp, Wg_words, Wg_scales
                     start=(g == 0),
                     stop=(g == A_PASSES - 1),
                 )
-            first_col = BANK * c + P * i
-            g_sb = results.tile([P, D], F32)
-            nc.vector.tensor_tensor(out=g_sb[:], in0=g_bank[:], in1=g_bias[:, first_col // COLS_PER_STEP, :], op=ADD)
-            nc.sync.dma_start(out=out_1[0, first_col : first_col + P, :], in_=g_sb[:])
+            t = c * STEPS_PER_CHUNK + u
+            if s == 0:
+                g_sb = results.tile([P, HANDS, D], F32)
+                pairs[1] = g_sb
+            g_sb = pairs[1]
+            nc.vector.tensor_tensor(out=g_sb[:, s, :], in0=g_bank[:], in1=g_bias[:, t, :], op=ADD)
+            if s == HANDS - 1:
+                step_rows = out_1[0, COLS_PER_STEP * t : COLS_PER_STEP * (t + 1), :]
+                nc.sync.dma_start(
+                    out=step_rows.rearrange("(m s) n -> m (s n)", s=HANDS), in_=g_sb[:].rearrange("p s n -> p (s n)")
+                )
 
         bias_bank = psum.tile([P, BANK], F32, tag="bank")
         nc.tensor.matmul(out=bias_bank[:, 0:P], lhsT=bias_rows[:], rhs=ident[:], start=True, stop=True)
@@ -229,13 +269,16 @@ def tile_nlgate_pa_kernel(tc, v, a, Wp_words, Wp_scales, bp, Wg_words, Wg_scales
         video_share(0, wp_codes, wp_planes)
         for t in range(STEPS // 2, STEPS, 2):
             nc.vector.tensor_copy(out=g_bias[:, t, :], in_=spreads[t][:])
+        grouped[0] = regroup(1, 0)
         for c in range(CHUNKS):
             more = c + 1 < CHUNKS
             if more:
-                grouped = {g: regroup(c + 1, g) for g in range(A_PASSES)}
+                grouped[1] = regroup(c + 1, 1)
             for i in range(N_TILES):
                 if more and i == N_TILES // 2:
-                    for g in range(A_PASSES):
+                    for g in reversed(range(A_PASSES)):
                         quantise(c + 1, g, grouped[g])
+                    if c + 2 < CHUNKS:
+                        grouped[0] = regroup(c + 2, 0)
                 phi_tile(c, i)
                 g_tile(c, i)

@@ -29,6 +29,7 @@ PIXEL_RUN = BANK // STEPS
 N_TILES = D // P
 Z_COPIES = P // STEPS
 STEPS_PER_CHUNK = BANK // COLS_PER_STEP
+WARM_MATMULS = 3
 HANDS = 2
 HAND_COLS = BANK // HANDS
 
@@ -175,7 +176,22 @@ def tile_nlgate_pa_kernel(tc, v, a, Wp_words, Wp_scales, bp, Wg_words, Wg_scales
             first_step = c * STEPS_PER_CHUNK
             by_step = phi_bank[:].rearrange("p (s u m) -> p u m s", s=HANDS, u=STEPS_PER_CHUNK)
             in_order = phi_sb[:, second, :].rearrange("p (u m s) -> p u m s", u=STEPS_PER_CHUNK, s=HANDS)
-            if i == N_TILES - 1:
+            final_chunk = c == CHUNKS - 1
+            if final_chunk and i == N_TILES - 1:
+                nc.vector.tensor_scalar(
+                    out=in_order[:, 0],
+                    in0=by_step[:, 0],
+                    scalar1=step_bias[:, 0, i, first_step : first_step + 1],
+                    scalar2=None,
+                    op0=ADD,
+                )
+                nc.scalar.activation(
+                    out=in_order[:, 1],
+                    in_=by_step[:, 1],
+                    func=IDENTITY,
+                    bias=step_bias[:, 0, i, first_step + 1 : first_step + 2],
+                )
+            elif i == N_TILES - 1:
                 nc.vector.tensor_tensor(
                     out=in_order,
                     in0=by_step,
@@ -191,7 +207,9 @@ def tile_nlgate_pa_kernel(tc, v, a, Wp_words, Wp_scales, bp, Wg_words, Wg_scales
                     nc.scalar.activation(
                         out=in_order[:, u], in_=by_step[:, u], func=IDENTITY, bias=step_bias[:, 0, i, t : t + 1]
                     )
-            if second == 1:
+            if final_chunk and k == 1:
+                nc.sync.dma_start(out=out_0[0, block, BANK * c : BANK * (c + 1)], in_=phi_sb[:, second, :])
+            elif second == 1:
                 two_blocks = out_0[0, 2 * P * k : 2 * P * (k + 1), BANK * c : BANK * (c + 1)]
                 nc.sync.dma_start(out=two_blocks.rearrange("(i p) w -> p i w", p=P), in_=phi_sb[:])
 
@@ -263,6 +281,10 @@ def tile_nlgate_pa_kernel(tc, v, a, Wp_words, Wp_scales, bp, Wg_words, Wg_scales
             elif t < STEPS // 2:
                 nc.vector.tensor_copy(out=g_bias[:, t, :], in_=spread[:])
 
+        warm = psum.tile([P, BANK], F32, tag="bank")
+        for w in range(WARM_MATMULS):
+            nc.tensor.matmul(out=warm[:], lhsT=ident[:], rhs=v_sb[:, 0, 0, 0:BANK], start=True, stop=True)
+
         grouped[0] = regroup(0, 0)
         for g in reversed(range(A_PASSES)):
             quantise(0, g, grouped[g])
@@ -274,11 +296,13 @@ def tile_nlgate_pa_kernel(tc, v, a, Wp_words, Wp_scales, bp, Wg_words, Wg_scales
             more = c + 1 < CHUNKS
             if more:
                 grouped[1] = regroup(c + 1, 1)
-            for i in range(N_TILES):
-                if more and i == N_TILES // 2:
+            kinds = (phi_tile, g_tile) if more else (g_tile, phi_tile)
+            for k in range(N_TILES // 2):
+                if more and k == 1:
                     for g in reversed(range(A_PASSES)):
                         quantise(c + 1, g, grouped[g])
                     if c + 2 < CHUNKS:
                         grouped[0] = regroup(c + 2, 0)
-                phi_tile(c, i)
-                g_tile(c, i)
+                for tile in kinds:
+                    tile(c, 2 * k)
+                    tile(c, 2 * k + 1)

@@ -83,10 +83,10 @@ def tile_nlgate_pa_kernel(tc, v, a, Wp_words, Wp_scales, bp, Wg_words, Wg_scales
         z_part = slice(A_PASSES, PASSES)
         a_part = slice(0, A_PASSES)
         for g in range(Z_PASSES):
-            for j in range(PACK):
+            for j in range(0, PACK, 2):
                 if (g, j) == (0, 2):
                     load_planes(wg_planes, Wg_scales)
-                nc.sync.dma_start(out=v_sb[:, g, j, :], in_=v_rows[g, :, j, :])
+                nc.sync.dma_start(out=v_sb[:, g, j : j + 2, :], in_=v_rows[g, :, j : j + 2, :])
         nc.sync.dma_start(out=wg_codes[:, z_part, :], in_=wg_rows[:, z_part, :])
         load_a(0)
         load_planes(wp_planes, Wp_scales)

@@ -29,7 +29,6 @@ PIXEL_RUN = BANK // STEPS
 N_TILES = D // P
 Z_COPIES = P // STEPS
 STEPS_PER_CHUNK = BANK // COLS_PER_STEP
-WARM_MATMULS = 3
 HANDS = 2
 HAND_COLS = BANK // HANDS
 
@@ -82,11 +81,10 @@ def tile_nlgate_pa_kernel(tc, v, a, Wp_words, Wp_scales, bp, Wg_words, Wg_scales
 
         z_part = slice(A_PASSES, PASSES)
         a_part = slice(0, A_PASSES)
-        for g in range(Z_PASSES):
-            for j in range(0, PACK, 2):
-                if (g, j) == (0, 2):
-                    load_planes(wg_planes, Wg_scales)
-                nc.sync.dma_start(out=v_sb[:, g, j : j + 2, :], in_=v_rows[g, :, j : j + 2, :])
+        for g, j, channels in ((0, 0, 2), (0, 2, 2), (1, 0, 2), (1, 2, 1), (1, 3, 1)):
+            if (g, j) == (0, 2):
+                load_planes(wg_planes, Wg_scales)
+            nc.sync.dma_start(out=v_sb[:, g, j : j + channels, :], in_=v_rows[g, :, j : j + channels, :])
         nc.sync.dma_start(out=wg_codes[:, z_part, :], in_=wg_rows[:, z_part, :])
         load_a(0)
         load_planes(wp_planes, Wp_scales)
@@ -268,28 +266,25 @@ def tile_nlgate_pa_kernel(tc, v, a, Wp_words, Wp_scales, bp, Wg_words, Wg_scales
         video_share(1, wg_codes, wg_planes)
         grouped = {1: regroup(0, 1)}
         g_bias = keep.tile([P, STEPS, D], F32)
-        spreads = []
-        for t in range(STEPS):
+        late_steps = list(range(2, STEPS, 2))
+        spreads = {}
+        for t in [0] + list(range(1, STEPS, 2)) + late_steps:
             spread = psum.tile([P, BANK], F32, tag="bank")
-            spreads.append(spread)
+            spreads[t] = spread
             for i in range(N_TILES):
                 nc.tensor.transpose(
                     spread[:, P * i : P * (i + 1)], step_bias[:, 1, i, t : t + 1].to_broadcast([P, P]), ident_f32[:]
                 )
             if t % 2 == 1:
                 nc.scalar.copy(out=g_bias[:, t, :], in_=spread[:])
-            elif t < STEPS // 2:
+            elif t == 0:
                 nc.vector.tensor_copy(out=g_bias[:, t, :], in_=spread[:])
-
-        warm = psum.tile([P, BANK], F32, tag="bank")
-        for w in range(WARM_MATMULS):
-            nc.tensor.matmul(out=warm[:], lhsT=ident[:], rhs=v_sb[:, 0, 0, 0:BANK], start=True, stop=True)
 
         grouped[0] = regroup(0, 0)
         for g in reversed(range(A_PASSES)):
             quantise(0, g, grouped[g])
         video_share(0, wp_codes, wp_planes)
-        for t in range(STEPS // 2, STEPS, 2):
+        for t in late_steps:
             nc.vector.tensor_copy(out=g_bias[:, t, :], in_=spreads[t][:])
         grouped[0] = regroup(1, 0)
         for c in range(CHUNKS):
@@ -297,12 +292,12 @@ def tile_nlgate_pa_kernel(tc, v, a, Wp_words, Wp_scales, bp, Wg_words, Wg_scales
             if more:
                 grouped[1] = regroup(c + 1, 1)
             kinds = (phi_tile, g_tile) if more else (g_tile, phi_tile)
-            for k in range(N_TILES // 2):
-                if more and k == 1:
+            tiles = [(tile, 2 * k + second) for k in range(N_TILES // 2) for tile in kinds for second in range(2)]
+            quantise_at = len(tiles) // 2 - (1 if c == 0 else 0)
+            for place, (tile, i) in enumerate(tiles):
+                if more and place == quantise_at:
                     for g in reversed(range(A_PASSES)):
                         quantise(c + 1, g, grouped[g])
                     if c + 2 < CHUNKS:
                         grouped[0] = regroup(c + 2, 0)
-                for tile in kinds:
-                    tile(c, 2 * k)
-                    tile(c, 2 * k + 1)
+                tile(c, i)

from contextlib import ExitStack

import concourse.mybir as mybir
from concourse.masks import make_identity

F32 = mybir.dt.float32
BF16 = mybir.dt.bfloat16
I32 = mybir.dt.int32
U8 = mybir.dt.uint8
FP8X4 = mybir.dt.float8_e4m3fn_x4
ADD = mybir.AluOpType.add
MULT = mybir.AluOpType.mult
IDENTITY = mybir.ActivationFunctionType.Identity

P = 128
PACK = 4
PASSES = 4
A_PASSES = 2
Z_PASSES = 2
STEPS = 8
PIXELS = 256
COLS = 2048
COLS_PER_STEP = COLS // STEPS
D = 512
BANK = 512
HALF = COLS // 2
CHUNKS = COLS // BANK
PIXEL_RUN = BANK // STEPS
N_TILES = D // P
Z_COPIES = P // STEPS
STEPS_PER_CHUNK = BANK // COLS_PER_STEP
HANDS = 2
HAND_COLS = BANK // HANDS

FLOPS = 2 * 2 * D * COLS * (PASSES * P * PACK)


def tile_nlgate_pa_kernel(tc, v, a, Wp_words, Wp_scales, bp, Wg_words, Wg_scales, bg, out_0, out_1):
    nc = tc.nc
    with ExitStack() as ctx:
        keep = ctx.enter_context(tc.tile_pool(name="keep", bufs=1))
        stage = ctx.enter_context(tc.tile_pool(name="stage", bufs=2))
        stage_0 = ctx.enter_context(tc.tile_pool(name="stage_0", bufs=1))
        results = ctx.enter_context(tc.tile_pool(name="results", bufs=6))
        psum = ctx.enter_context(tc.psum_pool(name="psum", bufs=8))
        ctx.enter_context(tc.manual_schedule())

        ident = keep.tile([P, P], BF16)
        make_identity(nc, ident[:])
        ident_f32 = keep.tile([P, P], F32)
        make_identity(nc, ident_f32[:])
        bias_rows = keep.tile([P, P], BF16)
        wp_planes = keep.tile([P, D], U8, align_bytes=64)
        wg_planes = keep.tile([P, D], U8, align_bytes=64)
        nc.vector.memset(wg_planes[:].bitcast(I32), 0)
        nc.vector.memset(bias_rows[:], 0.0)
        nc.vector.memset(wp_planes[:].bitcast(I32), 0)

        v_rows = v[0].rearrange("(g p j) t h w -> g p j (t h w)", p=P, j=PACK)
        a_rows = a[0].rearrange("(g p j) i f -> g p j (i f)", p=P, j=PACK)
        wp_rows = Wp_words.rearrange("g p n t -> p g (n t)").bitcast(I32)
        wg_rows = Wg_words.rearrange("g p n t -> p g (n t)").bitcast(I32)

        v_sb = keep.tile([P, Z_PASSES, PACK, STEPS * PIXELS], BF16)
        a_sb = keep.tile([P, 2, A_PASSES, PACK, HALF], BF16)
        wp_codes = keep.tile([P, PASSES, D], I32, align_bytes=64)
        wg_codes = keep.tile([P, PASSES, D], I32, align_bytes=64)

        nc.scalar.dma_start(out=bias_rows[0:N_TILES, :], in_=bp.rearrange("(r n) -> r n", n=P))
        nc.scalar.dma_start(out=bias_rows[N_TILES : 2 * N_TILES, :], in_=bg.rearrange("(r n) -> r n", n=P))
        def load_planes(planes, scales):
            for quad in range(4):
                nc.sync.dma_start(
                    out=planes[32 * quad : 32 * quad + 4 * PASSES, :].bitcast(I32),
                    in_=scales[:, 4 * quad : 4 * quad + 4, :].bitcast(I32),
                )

        def load_a(half):
            for g in reversed(range(A_PASSES)):
                nc.sync.dma_start(out=a_sb[:, half, g, :, :], in_=a_rows[g, :, :, HALF * half : HALF * (half + 1)])

        z_part = slice(A_PASSES, PASSES)
        a_part = slice(0, A_PASSES)
        for g, j, channels in ((0, 0, 2), (0, 2, 2), (1, 0, 2), (1, 2, 1), (1, 3, 1)):
            if (g, j) == (0, 2):
                load_planes(wg_planes, Wg_scales)
            nc.sync.dma_start(out=v_sb[:, g, j : j + channels, :], in_=v_rows[g, :, j : j + channels, :])
        nc.sync.dma_start(out=wg_codes[:, z_part, :], in_=wg_rows[:, z_part, :])
        load_a(0)
        load_planes(wp_planes, Wp_scales)
        nc.sync.dma_start(out=wp_codes[:, z_part, :], in_=wp_rows[:, z_part, :])
        nc.sync.dma_start(out=wp_codes[:, a_part, :], in_=wp_rows[:, a_part, :])
        nc.sync.dma_start(out=wg_codes[:, a_part, :], in_=wg_rows[:, a_part, :])
        load_a(1)

        z_sum = keep.tile([P, Z_PASSES, PACK, STEPS], F32)
        z_bf = keep.tile([P, Z_PASSES, STEPS, Z_COPIES, PACK], BF16, align_bytes=64)
        z_codes = keep.tile([P, Z_PASSES, P], I32, align_bytes=64)
        z_planes = keep.tile([P, Z_PASSES, P], U8, align_bytes=64)
        unused = keep.tile([P, PIXELS], BF16)
        for g in range(Z_PASSES):
            for t in range(STEPS):
                nc.scalar.activation(
                    out=unused[:],
                    in_=v_sb[:, g, 0, PIXELS * t : PIXELS * (t + 1)],
                    func=IDENTITY,
                    accum_out=z_sum[:, g, 0, t : t + 1],
                )
            for j in range(1, PACK):
                runs = v_sb[:, g, j, :].rearrange("p (t q r) -> p q t r", t=STEPS, r=PIXEL_RUN)
                folded = psum.tile([P, STEPS, PIXEL_RUN], F32, tag="bank")
                last = PIXELS // PIXEL_RUN - 1
                for q in range(last + 1):
                    nc.tensor.matmul(out=folded[:], lhsT=ident[:], rhs=runs[:, q], start=(q == 0), stop=(q == last))
                nc.vector.tensor_reduce(out=z_sum[:, g, j, :], in_=folded[:], axis=mybir.AxisListType.X, op=ADD)
            nc.vector.tensor_scalar(
                out=z_bf[:, g],
                in0=z_sum[:, g].rearrange("p j t -> p t j").unsqueeze(2).to_broadcast([P, STEPS, Z_COPIES, PACK]),
                scalar1=1.0 / PIXELS,
                scalar2=None,
                op0=MULT,
            )
            nc.vector.quantize_mx(
                out=z_codes[:, g, :].bitcast(FP8X4),
                scales=z_planes[:, g, :],
                in_=z_bf[:, g].rearrange("p t c j -> p (t c j)"),
            )

        a_codes = keep.tile([P, CHUNKS, A_PASSES, BANK], I32, align_bytes=64)
        a_planes = keep.tile([P, CHUNKS, A_PASSES, BANK], U8, align_bytes=64)

        def regroup(c, g):
            half, part = divmod(c, HALF // BANK)
            rows = a_sb[:, half, g, :, BANK * part : BANK * (part + 1)].rearrange("p j (m s) -> p s m j", s=HANDS)
            if g == 1:
                grouped = stage.tile([P, BANK, PACK], BF16, align_bytes=64)
                nc.scalar.copy(out=grouped[:].rearrange("p (s m) j -> p s m j", s=HANDS), in_=rows)
                return grouped
            grouped_0 = stage_0.tile([P, BANK, PACK], BF16, align_bytes=64)
            dealt = grouped_0[:].rearrange("p (s m) j -> p s m j", s=HANDS)
            if c == 0:
                nc.vector.tensor_copy(out=dealt, in_=rows)
            else:
                nc.gpsimd.tensor_scalar(out=dealt, in0=rows, scalar1=1.0, scalar2=0.0, op0=MULT, op1=ADD)
            return grouped_0

        def quantise(c, g, grouped):
            nc.vector.quantize_mx(
                out=a_codes[:, c, g, :].bitcast(FP8X4),
                scales=a_planes[:, c, g, :],
                in_=grouped[:].rearrange("p w j -> p (w j)"),
            )

        pairs = {}

        def phi_tile(c, i):
            block = slice(P * i, P * (i + 1))
            phi_bank = psum.tile([P, BANK], F32, tag="bank")
            for g in range(A_PASSES):
                nc.tensor.matmul_mx(
                    out=phi_bank[:],
                    lhsT=wp_codes[:, g, block].bitcast(FP8X4),
                    lhsT_scale=wp_planes[4 * g : P, block],
                    rhs=a_codes[:, c, g, :].bitcast(FP8X4),
                    rhs_scale=a_planes[:, c, g, :],
                    start=(g == 0),
                    stop=(g == A_PASSES - 1),
                )
            k, second = divmod(i, 2)
            if second == 0:
                phi_sb = results.tile([P, 2, BANK], F32)
                pairs[0] = phi_sb
            phi_sb = pairs[0]
            first_step = c * STEPS_PER_CHUNK
            by_step = phi_bank[:].rearrange("p (s u m) -> p u m s", s=HANDS, u=STEPS_PER_CHUNK)
            in_order = phi_sb[:, second, :].rearrange("p (u m s) -> p u m s", u=STEPS_PER_CHUNK, s=HANDS)
            final_chunk = c == CHUNKS - 1
            if final_chunk and i == N_TILES - 1:
                nc.vector.tensor_scalar(
                    out=in_order[:, 0],
                    in0=by_step[:, 0],
                    scalar1=step_bias[:, 0, i, first_step : first_step + 1],
                    scalar2=None,
                    op0=ADD,
                )
                nc.scalar.activation(
                    out=in_order[:, 1],
                    in_=by_step[:, 1],
                    func=IDENTITY,
                    bias=step_bias[:, 0, i, first_step + 1 : first_step + 2],
                )
            elif i == N_TILES - 1:
                nc.vector.tensor_tensor(
                    out=in_order,
                    in0=by_step,
                    in1=step_bias[:, 0, i, first_step : first_step + STEPS_PER_CHUNK]
                    .unsqueeze(2)
                    .unsqueeze(3)
                    .to_broadcast([P, STEPS_PER_CHUNK, P, HANDS]),
                    op=ADD,
                )
            else:
                for u in range(STEPS_PER_CHUNK):
                    t = first_step + u
                    nc.scalar.activation(
                        out=in_order[:, u], in_=by_step[:, u], func=IDENTITY, bias=step_bias[:, 0, i, t : t + 1]
                    )
            if final_chunk and k == 1:
                nc.sync.dma_start(out=out_0[0, block, BANK * c : BANK * (c + 1)], in_=phi_sb[:, second, :])
            elif second == 1:
                two_blocks = out_0[0, 2 * P * k : 2 * P * (k + 1), BANK * c : BANK * (c + 1)]
                nc.sync.dma_start(out=two_blocks.rearrange("(i p) w -> p i w", p=P), in_=phi_sb[:])

        def g_tile(c, i):
            u, s = divmod(i, HANDS)
            block = slice(HAND_COLS * s + P * u, HAND_COLS * s + P * (u + 1))
            g_bank = psum.tile([P, BANK], F32, tag="bank")
            for g in range(A_PASSES):
                nc.tensor.matmul_mx(
                    out=g_bank[:],
                    lhsT=a_codes[:, c, g, block].bitcast(FP8X4),
                    lhsT_scale=a_planes[:, c, g, block],
                    rhs=wg_codes[:, g, :].bitcast(FP8X4),
                    rhs_scale=wg_planes[4 * g : P, :],
                    start=(g == 0),
                    stop=(g == A_PASSES - 1),
                )
            t = c * STEPS_PER_CHUNK + u
            if s == 0:
                g_sb = results.tile([P, HANDS, D], F32)
                pairs[1] = g_sb
            g_sb = pairs[1]
            nc.vector.tensor_tensor(out=g_sb[:, s, :], in0=g_bank[:], in1=g_bias[:, t, :], op=ADD)
            if s == HANDS - 1:
                step_rows = out_1[0, COLS_PER_STEP * t : COLS_PER_STEP * (t + 1), :]
                nc.sync.dma_start(
                    out=step_rows.rearrange("(m s) n -> m (s n)", s=HANDS), in_=g_sb[:].rearrange("p s n -> p (s n)")
                )

        bias_bank = psum.tile([P, BANK], F32, tag="bank")
        nc.tensor.matmul(out=bias_bank[:, 0:P], lhsT=bias_rows[:], rhs=ident[:], start=True, stop=True)
        bias_col = keep.tile([P, 2, N_TILES], F32)
        nc.vector.tensor_copy(out=bias_col[:].rearrange("p b i -> p (b i)"), in_=bias_bank[:, 0 : 2 * N_TILES])
        step_bias = keep.tile([P, 2, N_TILES, STEPS], F32)

        def video_share(b, codes, planes):
            z_bank = psum.tile([P, N_TILES, P], F32, tag="bank")
            for i in range(N_TILES):
                n_cols = slice(P * i, P * (i + 1))
                for g in range(Z_PASSES):
                    nc.tensor.matmul_mx(
                        out=z_bank[:, i, :],
                        lhsT=codes[:, A_PASSES + g, n_cols].bitcast(FP8X4),
                        lhsT_scale=planes[4 * (A_PASSES + g) : P, n_cols],
                        rhs=z_codes[:, g, :].bitcast(FP8X4),
                        rhs_scale=z_planes[:, g, :],
                        start=(g == 0),
                        stop=(g == Z_PASSES - 1),
                    )
            nc.vector.tensor_tensor(
                out=step_bias[:, b],
                in0=z_bank[:].rearrange("p i (t c) -> p i t c", c=Z_COPIES)[:, :, :, 0],
                in1=bias_col[:, b, :].unsqueeze(2).to_broadcast([P, N_TILES, STEPS]),
                op=ADD,
            )
        video_share(1, wg_codes, wg_planes)
        grouped = {1: regroup(0, 1)}
        g_bias = keep.tile([P, STEPS, D], F32)
        late_steps = list(range(2, STEPS, 2))
        spreads = {}
        for t in [0] + list(range(1, STEPS, 2)) + late_steps:
            spread = psum.tile([P, BANK], F32, tag="bank")
            spreads[t] = spread
            for i in range(N_TILES):
                nc.tensor.transpose(
                    spread[:, P * i : P * (i + 1)], step_bias[:, 1, i, t : t + 1].to_broadcast([P, P]), ident_f32[:]
                )
            if t % 2 == 1:
                nc.scalar.copy(out=g_bias[:, t, :], in_=spread[:])
            elif t == 0:
                nc.vector.tensor_copy(out=g_bias[:, t, :], in_=spread[:])

        grouped[0] = regroup(0, 0)
        for g in reversed(range(A_PASSES)):
            quantise(0, g, grouped[g])
        video_share(0, wp_codes, wp_planes)
        for t in late_steps:
            nc.vector.tensor_copy(out=g_bias[:, t, :], in_=spreads[t][:])
        grouped[0] = regroup(1, 0)
        for c in range(CHUNKS):
            more = c + 1 < CHUNKS
            if more:
                grouped[1] = regroup(c + 1, 1)
            kinds = (phi_tile, g_tile) if more else (g_tile, phi_tile)
            tiles = [(tile, 2 * k + second) for k in range(N_TILES // 2) for tile in kinds for second in range(2)]
            quantise_at = len(tiles) // 2 - (1 if c == 0 else 0)
            for place, (tile, i) in enumerate(tiles):
                if more and place == quantise_at:
                    for g in reversed(range(A_PASSES)):
                        quantise(c + 1, g, grouped[g])
                    if c + 2 < CHUNKS:
                        grouped[0] = regroup(c + 2, 0)
                tile(c, i)
